import numpy as np
import ml_dtypes


def mxq(x, axis, fmt="e4m3"):
    dtype, down = {"e4m3": (ml_dtypes.float8_e4m3fn, 7), "e5m2": (ml_dtypes.float8_e5m2, 14)}[fmt]
    v = np.moveaxis(np.asarray(x, np.float32).astype(ml_dtypes.bfloat16).astype(np.float64), axis, -1)
    blocks = v.reshape(v.shape[:-1] + (-1, 32))
    amax = np.abs(blocks).max(-1, keepdims=True)
    byte = np.maximum(np.where(amax > 0, np.frexp(amax)[1] - 1 + 127, 0) - down, 1)
    scale = np.exp2(byte - 127.0)
    codes = (blocks / scale).astype(np.float32).astype(dtype).astype(np.float64)
    return np.moveaxis((codes * scale).reshape(v.shape), -1, axis)


WIDE = False


def mx_kscale(k):
    if not WIDE:
        return np.ones(k)
    levels = np.array([10, -10, 5, -5, 0])
    if k % 512:
        return np.exp2(np.random.permutation(np.resize(levels, k // 32))).repeat(32)
    a = np.empty((k // 512, 16))
    for p in range(k // 512):
        a[p, :8] = np.random.permutation(np.resize(levels, 8))
        for g in range(8):
            far = levels[np.abs(levels - a[p, g]) >= 10]
            a[p, g + 8] = far[np.random.randint(len(far))]
    return np.exp2(a.ravel()).repeat(32)


BF16 = ml_dtypes.bfloat16


def bf(x):
    return np.asarray(x, np.float32).astype(BF16)


def f64(x):
    return np.asarray(x).astype(np.float64)


B, LC, LL, LLAMA_DIM, DIM, HEADS, FF = 16, 77, 256, 512, 512, 16, 6144
EPS = 1e-5


def layernorm(x, g, b):
    m = x.mean(-1, keepdims=True)
    v = ((x - m) ** 2).mean(-1, keepdims=True)
    return (x - m) / np.sqrt(v + EPS) * g + b


def draw0():
    s, t = mx_kscale(LLAMA_DIM), mx_kscale(DIM)
    return {
        "llm_embed": bf(np.random.standard_normal((B, LL, LLAMA_DIM)) * s),
        "llm_proj_w": bf(np.random.standard_normal((DIM, LLAMA_DIM)) / np.sqrt(LLAMA_DIM) / s),
        "llm_proj_b": bf(0.1 * np.random.standard_normal(DIM)),
        "kvn_g": bf((1.0 + 0.1 * np.random.standard_normal(DIM)) * t),
        "kvn_b": bf(0.1 * np.random.standard_normal(DIM) * t),
        "q_w": bf(np.random.standard_normal((DIM, DIM)) / np.sqrt(DIM) / t),
        "q_b": bf(0.1 * np.random.standard_normal(DIM)),
    }


def core(llm_embed, llm_proj_w, llm_proj_b, kvn_g, kvn_b, q_w, q_b):
    llm = (mxq(f64(llm_embed), 2, "e4m3") @ mxq(f64(llm_proj_w), 1, "e4m3").T) + f64(llm_proj_b)
    llm_n = layernorm(llm, f64(kvn_g), f64(kvn_b))
    q = (mxq(llm_n, 2, "e4m3") @ mxq(f64(q_w), 1, "e4m3").T) + f64(q_b)
    return llm, q


def e4m3fn_bytes(y):
    return np.clip(np.asarray(y, np.float64), -448.0, 448.0).astype(np.float32).astype(ml_dtypes.float8_e4m3fn).view(np.uint8)


def e4m3fn_values(b):
    return np.asarray(b, np.uint8).view(ml_dtypes.float8_e4m3fn).astype(np.float64)


def setup_inputs():
    d = draw0()
    x0 = np.asarray(d['llm_embed']).astype(np.float64)
    s = (np.max(np.abs(x0), axis=(0, 1), keepdims=True) / 448.0).astype(np.float32)
    out = {}
    for k, v in d.items():
        if k == 'llm_embed':
            out['llm_embed_bytes'] = e4m3fn_bytes(x0 / s.astype(np.float64))
            out['llm_embed_scale'] = s
        else:
            out[k] = v
    return out


def reference(llm_embed_bytes, llm_embed_scale, llm_proj_w, llm_proj_b, kvn_g, kvn_b, q_w, q_b):
    return core(e4m3fn_values(llm_embed_bytes) * llm_embed_scale.astype(np.float64), llm_proj_w, llm_proj_b, kvn_g, kvn_b, q_w, q_b)

@@ -1,0 +1,247 @@
+from contextlib import ExitStack
+
+import concourse.mybir as mybir
+from concourse.masks import make_identity
+
+T, K, N = 4096, 512, 512
+EPS = 1e-5
+FLOPS = 2 * 2 * T * K * N
+
+F32 = mybir.dt.float32
+BF16 = mybir.dt.bfloat16
+U32 = mybir.dt.uint32
+U8 = mybir.dt.uint8
+FP8 = mybir.dt.float8_e4m3fn
+FP8X4 = mybir.dt.float8_e4m3fn_x4
+ACT = mybir.ActivationFunctionType
+ALU = mybir.AluOpType
+
+P = 128
+GROUP = 512
+UNIT = 256
+UNITS = T // UNIT
+
+
+def tile_crossfusion_pa_t_kernel(tc, x_bytes, x_scale, w1, b1, g, b, wq, qb, out_0, out_1):
+    nc = tc.nc
+    xv = x_bytes.rearrange("a l k -> (a l) k").rearrange("(G p j) k -> G p j k", p=P, j=4)
+    o0 = out_0.rearrange("a l k -> (a l) k").rearrange("(G p j) k -> G p j k", p=P, j=4)
+    o1 = out_1.rearrange("a l k -> (a l) k").rearrange("(G p j) k -> G p j k", p=P, j=4)
+
+    with ExitStack() as ctx:
+        keep = ctx.enter_context(tc.tile_pool(name="keep", bufs=1))
+        work = ctx.enter_context(tc.tile_pool(name="work", bufs=3))
+        outs = ctx.enter_context(tc.tile_pool(name="outs", bufs=4))
+        small = ctx.enter_context(tc.tile_pool(name="small", bufs=4))
+        px = ctx.enter_context(tc.psum_pool(name="px", bufs=2))
+        pz = ctx.enter_context(tc.psum_pool(name="pz", bufs=2))
+        pm = ctx.enter_context(tc.psum_pool(name="pm", bufs=4))
+
+        ident = keep.tile([P, P], F32)
+        s4 = keep.tile([P, 4], F32)
+        raw = [keep.tile([P, 4, K], U8, name="raw%d" % i, align_bytes=64) for i in range(T // GROUP)]
+        w1_sb = keep.tile([P, 4, K], BF16)
+        wq_sb = keep.tile([P, 4, K], BF16)
+        b1_bc = keep.tile([P, N], BF16)
+        qb_bc = keep.tile([P, N], BF16)
+        g_raw = keep.tile([P, 4], BF16)
+        b_raw = keep.tile([P, 4], BF16)
+        g4 = keep.tile([P, 4], F32)
+        b4 = keep.tile([P, 4], F32)
+        mhalf = keep.tile([P, 2], F32)
+        warm = keep.tile([P, 1], F32)
+        w_codes = [keep.tile([P, N], U32, name="w_codes%d" % i, align_bytes=64) for i in range(2)]
+        w_scales = [keep.tile([P, N], U8, name="w_scales%d" % i, align_bytes=64) for i in range(2)]
+
+        s = {}
+
+        def load_x(G):
+            nc.sync.dma_start(out=raw[G][:], in_=xv[G])
+
+        def word_transposes(words, rows):
+            xt = px.tile([P, 2, UNIT], F32, name="xt")
+            for i in range(2):
+                for h in range(2):
+                    nc.tensor.transpose(xt[:, h, P * i : P * (i + 1)], words[:, 256 * (rows + i) + h : 256 * (rows + i + 1) : 2], ident[:])
+            return xt
+
+        def weight(which, w_sb):
+            wg = keep.tile([P, 4 * N], BF16, name="wg%d" % which, align_bytes=64)
+            words = w_sb[:].rearrange("p c k -> p (c k)").bitcast(F32)
+            for half in range(2):
+                wt = word_transposes(words, 2 * half)
+                dst = wg[:, 1024 * half : 1024 * (half + 1)].bitcast(F32).rearrange("p (c h) -> p c h", h=2)
+                nc.vector.tensor_copy(out=dst, in_=wt[:].rearrange("p h c -> p c h"))
+            return wg
+
+        def weight_quant(which, wg):
+            nc.vector.quantize_mx(out=w_codes[which][:].bitcast(FP8X4), scales=w_scales[which][:], in_=wg[:])
+
+        def W(u):
+            xs = work.tile([P, 2 * K], BF16, name="xs", align_bytes=64)
+            src = raw[u // 2][:, 2 * (u % 2) : 2 * (u % 2) + 2, :].rearrange("p j k -> p (j k)").bitcast(FP8)
+            nc.scalar.copy(out=xs[:], in_=src)
+            s["xs", u] = xs
+
+        def XT(u):
+            s["xt", u] = word_transposes(s.pop(("xs", u))[:].bitcast(F32), 0)
+
+        def A(u):
+            xt = s.pop(("xt", u))
+            xg = work.tile([P, 4 * UNIT], BF16, name="xg", align_bytes=64)
+            nc.vector.tensor_tensor(
+                out=xg[:].rearrange("p (c h e) -> p c h e", h=2, e=2),
+                in0=xt[:].bitcast(BF16).rearrange("p h (c e) -> p c h e", e=2),
+                in1=s4[:].rearrange("p (h e) -> p h e", h=2).unsqueeze(1).to_broadcast([P, UNIT, 2, 2]),
+                op=ALU.mult,
+            )
+            s["xg", u] = xg
+
+        def QX(u):
+            xg = s.pop(("xg", u))
+            xc = work.tile([P, UNIT], U32, name="xc", align_bytes=64)
+            xsc = work.tile([P, UNIT], U8, name="xsc", align_bytes=64)
+            nc.vector.quantize_mx(out=xc[:].bitcast(FP8X4), scales=xsc[:], in_=xg[:])
+            s["xq", u] = (xc, xsc)
+
+        def MM(u, key, which, dst):
+            codes, scales = s.pop((key, u))
+            res = []
+            for i in range(2):
+                acc = pm.tile([P, N], F32, name="acc")
+                cols = slice(P * i, P * (i + 1))
+                nc.tensor.matmul_mx(out=acc[:], lhsT=codes[:, cols].bitcast(FP8X4), lhsT_scale=scales[:, cols], rhs=w_codes[which][:].bitcast(FP8X4), rhs_scale=w_scales[which][:], start=True, stop=True)
+                res.append(acc)
+            s[dst, u] = res
+
+        def T4(u):
+            accs = s.pop(("l", u))
+            llm = outs.tile([P, 2, N], F32, name="llm")
+            sums = small.tile([P, 2], F32, name="sums")
+            for i in range(2):
+                nc.vector.scalar_tensor_tensor(out=llm[:, i, :], in0=accs[i][:], scalar=1.0, in1=b1_bc[:], op0=ALU.mult, op1=ALU.add, accum_out=sums[:, i : i + 1])
+            nc.sync.dma_start(out=o0[u // 2][:, 2 * (u % 2) : 2 * (u % 2) + 2, :], in_=llm[:])
+            negmean = small.tile([P, 2], F32, name="negmean")
+            nc.scalar.activation(out=negmean[:], in_=sums[:], func=ACT.Copy, scale=-1.0 / N)
+            s["llm", u] = (llm, negmean)
+
+        def SQ(u):
+            llm, negmean = s["llm", u]
+            ssq = small.tile([P, 2], F32, name="ssq")
+            for i in range(2):
+                junk = work.tile([P, N], BF16, name="junk")
+                nc.scalar.activation(out=junk[:], in_=llm[:, i, :], func=ACT.Square, bias=negmean[:, i : i + 1], scale=1.0, accum_out=ssq[:, i : i + 1])
+            s["ssq", u] = ssq
+
+        def Z(u):
+            llm, negmean = s.pop(("llm", u))
+            ssq = s.pop(("ssq", u))
+            var = small.tile([P, 2], F32, name="var")
+            rstd = small.tile([P, 2], F32, name="rstd")
+            nc.gpsimd.tensor_scalar(out=var[:], in0=ssq[:], scalar1=1.0 / N, scalar2=EPS, op0=ALU.mult, op1=ALU.add)
+            nc.gpsimd.tensor_tensor(out=rstd[:], in0=var[:], in1=mhalf[:], op=ALU.pow)
+            z = work.tile([P, 2, 4, P], F32, name="z")
+            for i in range(2):
+                nc.gpsimd.tensor_scalar(out=z[:, i, :, :], in0=llm[:, i, :].rearrange("p (m t) -> p t m", t=4), scalar1=negmean[:, i : i + 1], scalar2=rstd[:, i : i + 1], op0=ALU.add, op1=ALU.mult)
+            s["z", u] = z
+
+        def ZT(u):
+            z = s.pop(("z", u))
+            res = []
+            for a in range(2):
+                zt = pz.tile([P, 2, UNIT], F32, name="zt")
+                for tt in range(2):
+                    for i in range(2):
+                        nc.tensor.transpose(zt[:, tt, P * i : P * (i + 1)], z[:, i, 2 * a + tt, :], ident[:])
+                res.append(zt)
+            s["zt", u] = res
+
+        def T7(u):
+            zts = s.pop(("zt", u))
+            yp = work.tile([P, 4, UNIT], BF16, name="yp", align_bytes=64)
+            for t in range(4):
+                nc.scalar.activation(out=yp[:, t, :], in_=zts[t // 2][:, t % 2, :], func=ACT.Identity, bias=b4[:, t : t + 1], scale=g4[:, t : t + 1])
+            s["yp", u] = yp
+
+        def T8(u):
+            yp = s.pop(("yp", u))
+            yg = work.tile([P, 4 * UNIT], BF16, name="yg", align_bytes=64)
+            dst, src = yg[:].rearrange("p (c t) -> p c t", t=4), yp[:].rearrange("p t c -> p c t")
+            nc.gpsimd.tensor_scalar(out=dst, in0=src, scalar1=1.0, scalar2=0.0, op0=ALU.mult, op1=ALU.add)
+            s["yg", u] = yg
+
+        def QY(u):
+            yg = s.pop(("yg", u))
+            yc = work.tile([P, UNIT], U32, name="yc", align_bytes=64)
+            ysc = work.tile([P, UNIT], U8, name="ysc", align_bytes=64)
+            nc.vector.quantize_mx(out=yc[:].bitcast(FP8X4), scales=ysc[:], in_=yg[:])
+            s["yq", u] = (yc, ysc)
+
+        def T9(u):
+            accs = s.pop(("q", u))
+            qo = outs.tile([P, 2, N], F32, name="qo")
+            for i in range(2):
+                nc.vector.tensor_tensor(out=qo[:, i, :], in0=accs[i][:], in1=qb_bc[:], op=ALU.add)
+            nc.sync.dma_start(out=o1[u // 2][:, 2 * (u % 2) : 2 * (u % 2) + 2, :], in_=qo[:])
+
+        def ok(u):
+            return 0 <= u < UNITS
+
+        with tc.manual_schedule():
+            nc.scalar.dma_start(out=s4[:], in_=x_scale.rearrange("a o (p t) -> p (a o t)", t=4))
+            load_x(0)
+            nc.sync.dma_start(out=w1_sb[:], in_=w1.rearrange("(c p) k -> p c k", p=P))
+            nc.scalar.dma_start(out=b1_bc[:], in_=b1.partition_broadcast(P))
+            load_x(1)
+            nc.sync.dma_start(out=wq_sb[:], in_=wq.rearrange("(c p) k -> p c k", p=P))
+            nc.scalar.dma_start(out=g_raw[:], in_=g.rearrange("(p t) -> p t", t=4))
+            nc.scalar.dma_start(out=b_raw[:], in_=b.rearrange("(p t) -> p t", t=4))
+            nc.scalar.dma_start(out=qb_bc[:], in_=qb.partition_broadcast(P))
+            for G in range(2, T // GROUP):
+                load_x(G)
+            make_identity(nc, ident[:])
+            nc.gpsimd.memset(mhalf[:], -0.5)
+            nc.gpsimd.memset(warm[:], 1.0)
+            nc.scalar.activation(out=warm[:], in_=warm[:], func=ACT.Square)
+            nc.gpsimd.tensor_copy(out=g4[:], in_=g_raw[:])
+            nc.gpsimd.tensor_copy(out=b4[:], in_=b_raw[:])
+            W(0)
+            XT(0)
+            wg1 = weight(0, w1_sb)
+            A(0)
+            weight_quant(0, wg1)
+            QX(0)
+            MM(0, "xq", 0, "l")
+            W(1)
+            XT(1)
+            A(1)
+            W(2)
+            XT(2)
+            wg2 = weight(1, wq_sb)
+            for i in range(UNITS + 3):
+                if ok(i - 2):
+                    T8(i - 2)
+                if ok(i + 3):
+                    W(i + 3)
+                if ok(i):
+                    T4(i)
+                    SQ(i)
+                if ok(i - 3):
+                    T9(i - 3)
+                if i == 0:
+                    weight_quant(1, wg2)
+                if ok(i + 1):
+                    QX(i + 1)
+                    MM(i + 1, "xq", 0, "l")
+                if ok(i + 2):
+                    A(i + 2)
+                if ok(i - 2):
+                    QY(i - 2)
+                    MM(i - 2, "yq", 1, "q")
+                if ok(i):
+                    Z(i)
+                if ok(i - 1):
+                    ZT(i - 1)
+                    T7(i - 1)
+                if ok(i + 3):
+                    XT(i + 3)

@@ -48,7 +48,7 @@ def tile_crossfusion_pa_t_kernel(tc, x_bytes, x_scale, w1, b1, g, b, wq, qb, out
         b_raw = keep.tile([P, 4], BF16)
         g4 = keep.tile([P, 4], F32)
         b4 = keep.tile([P, 4], F32)
-        mhalf = keep.tile([P, 2], F32)
+        eps = keep.tile([P, 1], F32)
         warm = keep.tile([P, 1], F32)
         w_codes = [keep.tile([P, N], U32, name="w_codes%d" % i, align_bytes=64) for i in range(2)]
         w_scales = [keep.tile([P, N], U8, name="w_scales%d" % i, align_bytes=64) for i in range(2)]
@@ -131,15 +131,13 @@ def tile_crossfusion_pa_t_kernel(tc, x_bytes, x_scale, w1, b1, g, b, wq, qb, out
             for i in range(2):
                 junk = work.tile([P, N], BF16, name="junk")
                 nc.scalar.activation(out=junk[:], in_=llm[:, i, :], func=ACT.Square, bias=negmean[:, i : i + 1], scale=1.0, accum_out=ssq[:, i : i + 1])
-            s["ssq", u] = ssq
+            rstd = small.tile([P, 2], F32, name="rstd")
+            nc.scalar.activation(out=rstd[:], in_=ssq[:], func=ACT.Abs_reciprocal_sqrt, bias=eps[:], scale=1.0 / N)
+            s["rstd", u] = rstd
 
         def Z(u):
             llm, negmean = s.pop(("llm", u))
-            ssq = s.pop(("ssq", u))
-            var = small.tile([P, 2], F32, name="var")
-            rstd = small.tile([P, 2], F32, name="rstd")
-            nc.gpsimd.tensor_scalar(out=var[:], in0=ssq[:], scalar1=1.0 / N, scalar2=EPS, op0=ALU.mult, op1=ALU.add)
-            nc.gpsimd.tensor_tensor(out=rstd[:], in0=var[:], in1=mhalf[:], op=ALU.pow)
+            rstd = s.pop(("rstd", u))
             z = work.tile([P, 2, 4, P], F32, name="z")
             for i in range(2):
                 nc.gpsimd.tensor_scalar(out=z[:, i, :, :], in0=llm[:, i, :].rearrange("p (m t) -> p t m", t=4), scalar1=negmean[:, i : i + 1], scalar2=rstd[:, i : i + 1], op0=ALU.add, op1=ALU.mult)
@@ -200,9 +198,9 @@ def tile_crossfusion_pa_t_kernel(tc, x_bytes, x_scale, w1, b1, g, b, wq, qb, out
             for G in range(2, T // GROUP):
                 load_x(G)
             make_identity(nc, ident[:])
-            nc.gpsimd.memset(mhalf[:], -0.5)
+            nc.gpsimd.memset(eps[:], EPS)
             nc.gpsimd.memset(warm[:], 1.0)
-            nc.scalar.activation(out=warm[:], in_=warm[:], func=ACT.Square)
+            nc.scalar.activation(out=warm[:], in_=warm[:], func=ACT.Abs_reciprocal_sqrt)
             nc.gpsimd.tensor_copy(out=g4[:], in_=g_raw[:])
             nc.gpsimd.tensor_copy(out=b4[:], in_=b_raw[:])
             W(0)

@@ -38,16 +38,16 @@ def tile_crossfusion_pa_t_kernel(tc, x_bytes, x_scale, w1, b1, g, b, wq, qb, out
         pm = ctx.enter_context(tc.psum_pool(name="pm", bufs=4))
 
         ident = keep.tile([P, P], F32)
-        s4 = keep.tile([P, 4], F32)
+        scale2 = keep.tile([P, 2, K], F32)
         raw = [keep.tile([P, 4, K], U8, name="raw%d" % i, align_bytes=64) for i in range(T // GROUP)]
         w1_sb = keep.tile([P, 4, K], BF16)
         wq_sb = keep.tile([P, 4, K], BF16)
         b1_bc = keep.tile([P, N], BF16)
         qb_bc = keep.tile([P, N], BF16)
-        g_raw = keep.tile([P, 4], BF16)
-        b_raw = keep.tile([P, 4], BF16)
-        g4 = keep.tile([P, 4], F32)
-        b4 = keep.tile([P, 4], F32)
+        gb_rows = keep.tile([P, N], BF16)
+        gb4 = keep.tile([P, 4, 2], F32)
+        wq_perm = keep.tile([P, 4, K], BF16)
+        ident_bf = keep.tile([P, P], BF16)
         eps = keep.tile([P, 1], F32)
         warm = keep.tile([P, 1], F32)
         w_codes = [keep.tile([P, N], U32, name="w_codes%d" % i, align_bytes=64) for i in range(2)]
@@ -71,30 +71,45 @@ def tile_crossfusion_pa_t_kernel(tc, x_bytes, x_scale, w1, b1, g, b, wq, qb, out
             for half in range(2):
                 wt = word_transposes(words, 2 * half)
                 dst = wg[:, 1024 * half : 1024 * (half + 1)].bitcast(F32).rearrange("p (c h) -> p c h", h=2)
-                nc.vector.tensor_copy(out=dst, in_=wt[:].rearrange("p h c -> p c h"))
+                nc.scalar.copy(out=dst, in_=wt[:].rearrange("p h c -> p c h"))
+            return wg
+
+        def weight_q():
+            wg = keep.tile([P, 4 * N], BF16, name="wg1", align_bytes=64)
+            gbt = px.tile([P, 4, P], BF16, name="xt")
+            for t in range(4):
+                nc.tensor.transpose(gbt[:, t, :], gb_rows[:, P * t : P * (t + 1)], ident_bf[:])
+            nc.scalar.copy(out=gb4[:], in_=gbt[:, :, 0:2])
+            for half in range(2):
+                wt = px.tile([P, 4, UNIT], BF16, name="xt")
+                for i in range(2):
+                    for t in range(4):
+                        nc.tensor.transpose(wt[:, t, P * i : P * (i + 1)], wq_perm[:, 2 * half + i, P * t : P * (t + 1)], ident_bf[:])
+                dst = wg[:, 1024 * half : 1024 * (half + 1)].rearrange("p (c t) -> p c t", t=4)
+                nc.scalar.copy(out=dst, in_=wt[:].rearrange("p t c -> p c t"))
             return wg
 
         def weight_quant(which, wg):
             nc.vector.quantize_mx(out=w_codes[which][:].bitcast(FP8X4), scales=w_scales[which][:], in_=wg[:])
 
-        def W(u):
+        def A(u):
             xs = work.tile([P, 2 * K], BF16, name="xs", align_bytes=64)
             src = raw[u // 2][:, 2 * (u % 2) : 2 * (u % 2) + 2, :].rearrange("p j k -> p (j k)").bitcast(FP8)
-            nc.scalar.copy(out=xs[:], in_=src)
+            if u < 2:
+                for i in range(2):
+                    half = slice(K * i, K * (i + 1))
+                    nc.vector.tensor_tensor(out=xs[:, half], in0=src[:, half], in1=scale2[:, 0, :], op=ALU.mult)
+            else:
+                nc.vector.tensor_tensor(out=xs[:], in0=src, in1=scale2[:].rearrange("p j k -> p (j k)"), op=ALU.mult)
             s["xs", u] = xs
 
         def XT(u):
             s["xt", u] = word_transposes(s.pop(("xs", u))[:].bitcast(F32), 0)
 
-        def A(u):
+        def T2(u):
             xt = s.pop(("xt", u))
             xg = work.tile([P, 4 * UNIT], BF16, name="xg", align_bytes=64)
-            nc.vector.tensor_tensor(
-                out=xg[:].rearrange("p (c h e) -> p c h e", h=2, e=2),
-                in0=xt[:].bitcast(BF16).rearrange("p h (c e) -> p c h e", e=2),
-                in1=s4[:].rearrange("p (h e) -> p h e", h=2).unsqueeze(1).to_broadcast([P, UNIT, 2, 2]),
-                op=ALU.mult,
-            )
+            nc.scalar.copy(out=xg[:].bitcast(F32).rearrange("p (c h) -> p c h", h=2), in_=xt[:].rearrange("p h c -> p c h"))
             s["xg", u] = xg
 
         def QX(u):
@@ -121,26 +136,33 @@ def tile_crossfusion_pa_t_kernel(tc, x_bytes, x_scale, w1, b1, g, b, wq, qb, out
             for i in range(2):
                 nc.vector.scalar_tensor_tensor(out=llm[:, i, :], in0=accs[i][:], scalar=1.0, in1=b1_bc[:], op0=ALU.mult, op1=ALU.add, accum_out=sums[:, i : i + 1])
             nc.sync.dma_start(out=o0[u // 2][:, 2 * (u % 2) : 2 * (u % 2) + 2, :], in_=llm[:])
+            s["llm", u] = (llm, sums)
+
+        def NM(u):
+            llm, sums = s.pop(("llm", u))
             negmean = small.tile([P, 2], F32, name="negmean")
             nc.scalar.activation(out=negmean[:], in_=sums[:], func=ACT.Copy, scale=-1.0 / N)
-            s["llm", u] = (llm, negmean)
+            s["c", u] = (llm, negmean)
 
         def SQ(u):
-            llm, negmean = s["llm", u]
+            llm, negmean = s["c", u]
             ssq = small.tile([P, 2], F32, name="ssq")
             for i in range(2):
                 junk = work.tile([P, N], BF16, name="junk")
                 nc.scalar.activation(out=junk[:], in_=llm[:, i, :], func=ACT.Square, bias=negmean[:, i : i + 1], scale=1.0, accum_out=ssq[:, i : i + 1])
+            s["ssq", u] = ssq
+
+        def RS(u):
             rstd = small.tile([P, 2], F32, name="rstd")
-            nc.scalar.activation(out=rstd[:], in_=ssq[:], func=ACT.Abs_reciprocal_sqrt, bias=eps[:], scale=1.0 / N)
+            nc.scalar.activation(out=rstd[:], in_=s.pop(("ssq", u))[:], func=ACT.Abs_reciprocal_sqrt, bias=eps[:], scale=1.0 / N)
             s["rstd", u] = rstd
 
         def Z(u):
-            llm, negmean = s.pop(("llm", u))
+            llm, negmean = s.pop(("c", u))
             rstd = s.pop(("rstd", u))
             z = work.tile([P, 2, 4, P], F32, name="z")
             for i in range(2):
-                nc.gpsimd.tensor_scalar(out=z[:, i, :, :], in0=llm[:, i, :].rearrange("p (m t) -> p t m", t=4), scalar1=negmean[:, i : i + 1], scalar2=rstd[:, i : i + 1], op0=ALU.add, op1=ALU.mult)
+                nc.gpsimd.tensor_scalar(out=z[:, i, :, :].rearrange("p t (b r) -> p t b r", r=8), in0=llm[:, i, :].rearrange("p (b t r) -> p t b r", t=4, r=8), scalar1=negmean[:, i : i + 1], scalar2=rstd[:, i : i + 1], op0=ALU.add, op1=ALU.mult)
             s["z", u] = z
 
         def ZT(u):
@@ -154,18 +176,25 @@ def tile_crossfusion_pa_t_kernel(tc, x_bytes, x_scale, w1, b1, g, b, wq, qb, out
                 res.append(zt)
             s["zt", u] = res
 
-        def T7(u):
-            zts = s.pop(("zt", u))
-            yp = work.tile([P, 4, UNIT], BF16, name="yp", align_bytes=64)
-            for t in range(4):
-                nc.scalar.activation(out=yp[:, t, :], in_=zts[t // 2][:, t % 2, :], func=ACT.Identity, bias=b4[:, t : t + 1], scale=g4[:, t : t + 1])
-            s["yp", u] = yp
+        def T7(u, ts):
+            zts = s["zt", u]
+            if 0 in ts:
+                s["yp", u] = work.tile([P, 4, UNIT], BF16, name="yp", align_bytes=64)
+            yp = s["yp", u]
+            for t in ts:
+                nc.scalar.activation(out=yp[:, t, :], in_=zts[t // 2][:, t % 2, :], func=ACT.Identity, bias=gb4[:, t, 1:2], scale=gb4[:, t, 0:1])
+
+        def on_scalar(u):
+            return u % 4 != 3 and u < 14
 
         def T8(u):
             yp = s.pop(("yp", u))
             yg = work.tile([P, 4 * UNIT], BF16, name="yg", align_bytes=64)
             dst, src = yg[:].rearrange("p (c t) -> p c t", t=4), yp[:].rearrange("p t c -> p c t")
-            nc.gpsimd.tensor_scalar(out=dst, in0=src, scalar1=1.0, scalar2=0.0, op0=ALU.mult, op1=ALU.add)
+            if on_scalar(u):
+                nc.scalar.copy(out=dst, in_=src)
+            else:
+                nc.vector.tensor_copy(out=dst, in_=src)
             s["yg", u] = yg
 
         def QY(u):
@@ -186,14 +215,15 @@ def tile_crossfusion_pa_t_kernel(tc, x_bytes, x_scale, w1, b1, g, b, wq, qb, out
             return 0 <= u < UNITS
 
         with tc.manual_schedule():
-            nc.scalar.dma_start(out=s4[:], in_=x_scale.rearrange("a o (p t) -> p (a o t)", t=4))
+            nc.scalar.dma_start(out=scale2[:, 0, :], in_=x_scale.rearrange("a o k -> (a o k)").partition_broadcast(P))
             load_x(0)
             nc.sync.dma_start(out=w1_sb[:], in_=w1.rearrange("(c p) k -> p c k", p=P))
             nc.scalar.dma_start(out=b1_bc[:], in_=b1.partition_broadcast(P))
             load_x(1)
             nc.sync.dma_start(out=wq_sb[:], in_=wq.rearrange("(c p) k -> p c k", p=P))
-            nc.scalar.dma_start(out=g_raw[:], in_=g.rearrange("(p t) -> p t", t=4))
-            nc.scalar.dma_start(out=b_raw[:], in_=b.rearrange("(p t) -> p t", t=4))
+            nc.gpsimd.memset(gb_rows[:], 0.0)
+            for row, vec in ((0, g), (1, b)):
+                nc.scalar.dma_start(out=gb_rows[row : row + 1, :].rearrange("o (t b r) -> o t b r", t=4, r=8), in_=vec.rearrange("(o b t r) -> o t b r", o=1, t=4, r=8))
             nc.scalar.dma_start(out=qb_bc[:], in_=qb.partition_broadcast(P))
             for G in range(2, T // GROUP):
                 load_x(G)
@@ -201,45 +231,56 @@ def tile_crossfusion_pa_t_kernel(tc, x_bytes, x_scale, w1, b1, g, b, wq, qb, out
             nc.gpsimd.memset(eps[:], EPS)
             nc.gpsimd.memset(warm[:], 1.0)
             nc.scalar.activation(out=warm[:], in_=warm[:], func=ACT.Abs_reciprocal_sqrt)
-            nc.gpsimd.tensor_copy(out=g4[:], in_=g_raw[:])
-            nc.gpsimd.tensor_copy(out=b4[:], in_=b_raw[:])
-            W(0)
-            XT(0)
+            make_identity(nc, ident_bf[:])
+            for c in range(4):
+                nc.gpsimd.tensor_scalar(
+                    out=wq_perm[:, c, :].rearrange("p (t b r) -> p t b r", t=4, r=8),
+                    in0=wq_sb[:, c, :].rearrange("p (b t r) -> p t b r", t=4, r=8),
+                    scalar1=1.0, scalar2=0.0, op0=ALU.mult, op1=ALU.add)
             wg1 = weight(0, w1_sb)
             A(0)
+            XT(0)
+            T2(0)
+            A(1)
+            XT(1)
+            T2(1)
+            nc.scalar.copy(out=scale2[:, 1, :], in_=scale2[:, 0, :])
             weight_quant(0, wg1)
             QX(0)
             MM(0, "xq", 0, "l")
-            W(1)
-            XT(1)
-            A(1)
-            W(2)
+            A(2)
             XT(2)
-            wg2 = weight(1, wq_sb)
             for i in range(UNITS + 3):
-                if ok(i - 2):
-                    T8(i - 2)
-                if ok(i + 3):
-                    W(i + 3)
                 if ok(i):
                     T4(i)
+                if ok(i - 2):
+                    T8(i - 2)
+                if ok(i + 2):
+                    T2(i + 2)
+                if i == 0:
+                    wg2 = weight_q()
+                if ok(i - 1):
+                    ZT(i - 1)
+                if ok(i):
+                    NM(i)
                     SQ(i)
+                if ok(i - 1):
+                    T7(i - 1, (0,))
+                if ok(i):
+                    RS(i)
+                    Z(i)
+                if ok(i - 1):
+                    T7(i - 1, (1, 2, 3))
                 if ok(i - 3):
                     T9(i - 3)
-                if i == 0:
-                    weight_quant(1, wg2)
                 if ok(i + 1):
                     QX(i + 1)
                     MM(i + 1, "xq", 0, "l")
-                if ok(i + 2):
-                    A(i + 2)
+                if i == 0:
+                    weight_quant(1, wg2)
+                if ok(i + 3):
+                    A(i + 3)
+                    XT(i + 3)
                 if ok(i - 2):
                     QY(i - 2)
                     MM(i - 2, "yq", 1, "q")
-                if ok(i):
-                    Z(i)
-                if ok(i - 1):
-                    ZT(i - 1)
-                    T7(i - 1)
-                if ok(i + 3):
-                    XT(i + 3)

@@ -42,6 +42,11 @@ def tile_crossfusion_pa_t_kernel(tc, x_bytes, x_scale, w1, b1, g, b, wq, qb, out
         raw = [keep.tile([P, 4, K], U8, name="raw%d" % i, align_bytes=64) for i in range(T // GROUP)]
         w1_sb = keep.tile([P, 4, K], BF16)
         wq_sb = keep.tile([P, 4, K], BF16)
+        s_col = keep.tile([P, 4], F32)
+        b1_raw = keep.tile([P, 4], BF16)
+        qb_raw = keep.tile([P, 4], BF16)
+        b1_col = keep.tile([P, 4], F32)
+        qb_col = keep.tile([P, 4], F32)
         b1_bc = keep.tile([P, N], BF16)
         qb_bc = keep.tile([P, N], BF16)
         gb_rows = keep.tile([P, N], BF16)
@@ -58,36 +63,40 @@ def tile_crossfusion_pa_t_kernel(tc, x_bytes, x_scale, w1, b1, g, b, wq, qb, out
         def load_x(G):
             nc.sync.dma_start(out=raw[G][:], in_=xv[G])
 
-        def word_transposes(words, rows):
-            xt = px.tile([P, 2, UNIT], F32, name="xt")
+        def spread(col):
+            bt = pm.tile([P, 4, P], F32, name="acc")
+            for t in range(4):
+                nc.tensor.transpose(bt[:, t, :], col[:, t : t + 1].to_broadcast([P, P]), ident[:])
+            return bt[:].rearrange("p t m -> p m t")
+
+        def word_transposes(words, rows, xt):
             for i in range(2):
                 for h in range(2):
                     nc.tensor.transpose(xt[:, h, P * i : P * (i + 1)], words[:, 256 * (rows + i) + h : 256 * (rows + i + 1) : 2], ident[:])
             return xt
 
-        def weight(which, w_sb):
-            wg = keep.tile([P, 4 * N], BF16, name="wg%d" % which, align_bytes=64)
-            words = w_sb[:].rearrange("p c k -> p (c k)").bitcast(F32)
-            for half in range(2):
-                wt = word_transposes(words, 2 * half)
-                dst = wg[:, 1024 * half : 1024 * (half + 1)].bitcast(F32).rearrange("p (c h) -> p c h", h=2)
-                nc.scalar.copy(out=dst, in_=wt[:].rearrange("p h c -> p c h"))
-            return wg
+        def w1_half(half):
+            if half == 0:
+                s["wg1"] = keep.tile([P, 4 * N], BF16, name="wg0", align_bytes=64)
+            wt = pm.tile([P, 2, UNIT], F32, name="acc")
+            word_transposes(w1_sb[:].rearrange("p c k -> p (c k)").bitcast(F32), 2 * half, wt)
+            dst = s["wg1"][:, 1024 * half : 1024 * (half + 1)].bitcast(F32).rearrange("p (c h) -> p c h", h=2)
+            copy = nc.scalar.copy if half == 0 else nc.vector.tensor_copy
+            copy(out=dst, in_=wt[:].rearrange("p h c -> p c h"))
 
-        def weight_q():
-            wg = keep.tile([P, 4 * N], BF16, name="wg1", align_bytes=64)
-            gbt = px.tile([P, 4, P], BF16, name="xt")
-            for t in range(4):
-                nc.tensor.transpose(gbt[:, t, :], gb_rows[:, P * t : P * (t + 1)], ident_bf[:])
-            nc.scalar.copy(out=gb4[:], in_=gbt[:, :, 0:2])
-            for half in range(2):
-                wt = px.tile([P, 4, UNIT], BF16, name="xt")
-                for i in range(2):
-                    for t in range(4):
-                        nc.tensor.transpose(wt[:, t, P * i : P * (i + 1)], wq_perm[:, 2 * half + i, P * t : P * (t + 1)], ident_bf[:])
-                dst = wg[:, 1024 * half : 1024 * (half + 1)].rearrange("p (c t) -> p c t", t=4)
-                nc.scalar.copy(out=dst, in_=wt[:].rearrange("p t c -> p c t"))
-            return wg
+        def wq_half(half):
+            if half == 0:
+                s["wgq"] = keep.tile([P, 4 * N], BF16, name="wg1", align_bytes=64)
+                gbt = px.tile([P, 4, P], BF16, name="xt")
+                for t in range(4):
+                    nc.tensor.transpose(gbt[:, t, :], gb_rows[:, P * t : P * (t + 1)], ident_bf[:])
+                nc.scalar.copy(out=gb4[:], in_=gbt[:, :, 0:2])
+            wt = px.tile([P, 4, UNIT], BF16, name="xt")
+            for i in range(2):
+                for t in range(4):
+                    nc.tensor.transpose(wt[:, t, P * i : P * (i + 1)], wq_perm[:, 2 * half + i, P * t : P * (t + 1)], ident_bf[:])
+            dst = s["wgq"][:, 1024 * half : 1024 * (half + 1)].rearrange("p (c t) -> p c t", t=4)
+            nc.scalar.copy(out=dst, in_=wt[:].rearrange("p t c -> p c t"))
 
         def weight_quant(which, wg):
             nc.vector.quantize_mx(out=w_codes[which][:].bitcast(FP8X4), scales=w_scales[which][:], in_=wg[:])
@@ -104,7 +113,8 @@ def tile_crossfusion_pa_t_kernel(tc, x_bytes, x_scale, w1, b1, g, b, wq, qb, out
             s["xs", u] = xs
 
         def XT(u):
-            s["xt", u] = word_transposes(s.pop(("xs", u))[:].bitcast(F32), 0)
+            xt = px.tile([P, 2, UNIT], F32, name="xt")
+            s["xt", u] = word_transposes(s.pop(("xs", u))[:].bitcast(F32), 0, xt)
 
         def T2(u):
             xt = s.pop(("xt", u))
@@ -138,28 +148,24 @@ def tile_crossfusion_pa_t_kernel(tc, x_bytes, x_scale, w1, b1, g, b, wq, qb, out
             nc.sync.dma_start(out=o0[u // 2][:, 2 * (u % 2) : 2 * (u % 2) + 2, :], in_=llm[:])
             s["llm", u] = (llm, sums)
 
-        def NM(u):
-            llm, sums = s.pop(("llm", u))
-            negmean = small.tile([P, 2], F32, name="negmean")
-            nc.scalar.activation(out=negmean[:], in_=sums[:], func=ACT.Copy, scale=-1.0 / N)
-            s["c", u] = (llm, negmean)
-
         def SQ(u):
-            llm, negmean = s["c", u]
+            llm, sums = s["llm", u]
             ssq = small.tile([P, 2], F32, name="ssq")
             for i in range(2):
                 junk = work.tile([P, N], BF16, name="junk")
-                nc.scalar.activation(out=junk[:], in_=llm[:, i, :], func=ACT.Square, bias=negmean[:, i : i + 1], scale=1.0, accum_out=ssq[:, i : i + 1])
+                nc.scalar.activation(out=junk[:], in_=llm[:, i, :], func=ACT.Square, bias=sums[:, i : i + 1], scale=-float(N), accum_out=ssq[:, i : i + 1])
             s["ssq", u] = ssq
 
         def RS(u):
             rstd = small.tile([P, 2], F32, name="rstd")
-            nc.scalar.activation(out=rstd[:], in_=s.pop(("ssq", u))[:], func=ACT.Abs_reciprocal_sqrt, bias=eps[:], scale=1.0 / N)
+            nc.scalar.activation(out=rstd[:], in_=s.pop(("ssq", u))[:], func=ACT.Abs_reciprocal_sqrt, bias=eps[:], scale=1.0 / N**3)
             s["rstd", u] = rstd
 
         def Z(u):
-            llm, negmean = s.pop(("c", u))
+            llm, sums = s.pop(("llm", u))
             rstd = s.pop(("rstd", u))
+            negmean = small.tile([P, 2], F32, name="negmean")
+            nc.gpsimd.tensor_scalar(out=negmean[:], in0=sums[:], scalar1=-1.0 / N, scalar2=0.0, op0=ALU.mult, op1=ALU.add)
             z = work.tile([P, 2, 4, P], F32, name="z")
             for i in range(2):
                 nc.gpsimd.tensor_scalar(out=z[:, i, :, :].rearrange("p t (b r) -> p t b r", r=8), in0=llm[:, i, :].rearrange("p (b t r) -> p t b r", t=4, r=8), scalar1=negmean[:, i : i + 1], scalar2=rstd[:, i : i + 1], op0=ALU.add, op1=ALU.mult)
@@ -185,7 +191,7 @@ def tile_crossfusion_pa_t_kernel(tc, x_bytes, x_scale, w1, b1, g, b, wq, qb, out
                 nc.scalar.activation(out=yp[:, t, :], in_=zts[t // 2][:, t % 2, :], func=ACT.Identity, bias=gb4[:, t, 1:2], scale=gb4[:, t, 0:1])
 
         def on_scalar(u):
-            return u % 4 != 3 and u < 14
+            return u % 2 == 1 and u < 13
 
         def T8(u):
             yp = s.pop(("yp", u))
@@ -209,78 +215,88 @@ def tile_crossfusion_pa_t_kernel(tc, x_bytes, x_scale, w1, b1, g, b, wq, qb, out
             qo = outs.tile([P, 2, N], F32, name="qo")
             for i in range(2):
                 nc.vector.tensor_tensor(out=qo[:, i, :], in0=accs[i][:], in1=qb_bc[:], op=ALU.add)
-            nc.sync.dma_start(out=o1[u // 2][:, 2 * (u % 2) : 2 * (u % 2) + 2, :], in_=qo[:])
+                if u == UNITS - 1:
+                    nc.sync.dma_start(out=o1[u // 2][:, 2 * (u % 2) + i, :], in_=qo[:, i, :])
+            if u < UNITS - 1:
+                nc.sync.dma_start(out=o1[u // 2][:, 2 * (u % 2) : 2 * (u % 2) + 2, :], in_=qo[:])
 
         def ok(u):
             return 0 <= u < UNITS
 
         with tc.manual_schedule():
-            nc.scalar.dma_start(out=scale2[:, 0, :], in_=x_scale.rearrange("a o k -> (a o k)").partition_broadcast(P))
+            nc.scalar.dma_start(out=s_col[:], in_=x_scale.rearrange("a o (p t) -> p (a o t)", t=4))
+            nc.scalar.dma_start(out=b1_raw[:], in_=b1.rearrange("(p t) -> p t", t=4))
+            nc.scalar.dma_start(out=qb_raw[:], in_=qb.rearrange("(p t) -> p t", t=4))
             load_x(0)
             nc.sync.dma_start(out=w1_sb[:], in_=w1.rearrange("(c p) k -> p c k", p=P))
-            nc.scalar.dma_start(out=b1_bc[:], in_=b1.partition_broadcast(P))
             load_x(1)
             nc.sync.dma_start(out=wq_sb[:], in_=wq.rearrange("(c p) k -> p c k", p=P))
+            make_identity(nc, ident[:])
+            nc.gpsimd.memset(warm[:], 1.0)
             nc.gpsimd.memset(gb_rows[:], 0.0)
+            nc.gpsimd.memset(eps[:], EPS)
+            make_identity(nc, ident_bf[:])
             for row, vec in ((0, g), (1, b)):
-                nc.scalar.dma_start(out=gb_rows[row : row + 1, :].rearrange("o (t b r) -> o t b r", t=4, r=8), in_=vec.rearrange("(o b t r) -> o t b r", o=1, t=4, r=8))
-            nc.scalar.dma_start(out=qb_bc[:], in_=qb.partition_broadcast(P))
+                nc.sync.dma_start(out=gb_rows[row : row + 1, :].rearrange("o (t b r) -> o t b r", t=4, r=8), in_=vec.rearrange("(o b t r) -> o t b r", o=1, t=4, r=8))
             for G in range(2, T // GROUP):
                 load_x(G)
-            make_identity(nc, ident[:])
-            nc.gpsimd.memset(eps[:], EPS)
-            nc.gpsimd.memset(warm[:], 1.0)
             nc.scalar.activation(out=warm[:], in_=warm[:], func=ACT.Abs_reciprocal_sqrt)
-            make_identity(nc, ident_bf[:])
+            nc.gpsimd.tensor_copy(out=b1_col[:], in_=b1_raw[:])
+            nc.gpsimd.tensor_copy(out=qb_col[:], in_=qb_raw[:])
             for c in range(4):
                 nc.gpsimd.tensor_scalar(
                     out=wq_perm[:, c, :].rearrange("p (t b r) -> p t b r", t=4, r=8),
                     in0=wq_sb[:, c, :].rearrange("p (b t r) -> p t b r", t=4, r=8),
                     scalar1=1.0, scalar2=0.0, op0=ALU.mult, op1=ALU.add)
-            wg1 = weight(0, w1_sb)
+            nc.scalar.copy(out=scale2[:, 0, :].rearrange("p (m t) -> p m t", t=4), in_=spread(s_col))
+            w1_half(0)
             A(0)
+            w1_half(1)
+            b1_spread = spread(b1_col)
             XT(0)
             T2(0)
+            nc.scalar.copy(out=b1_bc[:].rearrange("p (m t) -> p m t", t=4), in_=b1_spread)
+            weight_quant(0, s.pop("wg1"))
+            QX(0)
+            MM(0, "xq", 0, "l")
+            nc.scalar.copy(out=qb_bc[:].rearrange("p (m t) -> p m t", t=4), in_=spread(qb_col))
+            nc.scalar.copy(out=scale2[:, 1, :], in_=scale2[:, 0, :])
             A(1)
             XT(1)
             T2(1)
-            nc.scalar.copy(out=scale2[:, 1, :], in_=scale2[:, 0, :])
-            weight_quant(0, wg1)
-            QX(0)
-            MM(0, "xq", 0, "l")
-            A(2)
-            XT(2)
             for i in range(UNITS + 3):
                 if ok(i):
                     T4(i)
+                if i == 0:
+                    A(2)
+                    XT(2)
                 if ok(i - 2):
                     T8(i - 2)
-                if ok(i + 2):
-                    T2(i + 2)
-                if i == 0:
-                    wg2 = weight_q()
                 if ok(i - 1):
                     ZT(i - 1)
-                if ok(i):
-                    NM(i)
-                    SQ(i)
-                if ok(i - 1):
-                    T7(i - 1, (0,))
-                if ok(i):
-                    RS(i)
-                    Z(i)
-                if ok(i - 1):
-                    T7(i - 1, (1, 2, 3))
-                if ok(i - 3):
-                    T9(i - 3)
                 if ok(i + 1):
                     QX(i + 1)
-                    MM(i + 1, "xq", 0, "l")
-                if i == 0:
-                    weight_quant(1, wg2)
                 if ok(i + 3):
                     A(i + 3)
-                    XT(i + 3)
+                if ok(i + 1):
+                    MM(i + 1, "xq", 0, "l")
+                if ok(i):
+                    SQ(i)
+                    RS(i)
+                if i == 2:
+                    weight_quant(1, s.pop("wgq"))
                 if ok(i - 2):
                     QY(i - 2)
                     MM(i - 2, "yq", 1, "q")
+                if ok(i + 3):
+                    XT(i + 3)
+                if ok(i):
+                    Z(i)
+                if ok(i - 3):
+                    T9(i - 3)
+                if ok(i - 1):
+                    T7(i - 1, (0, 1, 2, 3))
+                if ok(i + 2) and i >= 0:
+                    T2(i + 2)
+                if i < 2:
+                    wq_half(i)

from contextlib import ExitStack

import concourse.mybir as mybir
from concourse.masks import make_identity

T, K, N = 4096, 512, 512
EPS = 1e-5
FLOPS = 2 * 2 * T * K * N

F32 = mybir.dt.float32
BF16 = mybir.dt.bfloat16
U32 = mybir.dt.uint32
U8 = mybir.dt.uint8
FP8 = mybir.dt.float8_e4m3fn
FP8X4 = mybir.dt.float8_e4m3fn_x4
ACT = mybir.ActivationFunctionType
ALU = mybir.AluOpType

P = 128
GROUP = 512
UNIT = 256
UNITS = T // UNIT


def tile_crossfusion_pa_t_kernel(tc, x_bytes, x_scale, w1, b1, g, b, wq, qb, out_0, out_1):
    nc = tc.nc
    xv = x_bytes.rearrange("a l k -> (a l) k").rearrange("(G p j) k -> G p j k", p=P, j=4)
    o0 = out_0.rearrange("a l k -> (a l) k").rearrange("(G p j) k -> G p j k", p=P, j=4)
    o1 = out_1.rearrange("a l k -> (a l) k").rearrange("(G p j) k -> G p j k", p=P, j=4)

    with ExitStack() as ctx:
        keep = ctx.enter_context(tc.tile_pool(name="keep", bufs=1))
        work = ctx.enter_context(tc.tile_pool(name="work", bufs=3))
        outs = ctx.enter_context(tc.tile_pool(name="outs", bufs=4))
        small = ctx.enter_context(tc.tile_pool(name="small", bufs=4))
        px = ctx.enter_context(tc.psum_pool(name="px", bufs=2))
        pz = ctx.enter_context(tc.psum_pool(name="pz", bufs=2))
        pm = ctx.enter_context(tc.psum_pool(name="pm", bufs=4))

        ident = keep.tile([P, P], F32)
        scale2 = keep.tile([P, 2, K], F32)
        raw = [keep.tile([P, 4, K], U8, name="raw%d" % i, align_bytes=64) for i in range(T // GROUP)]
        w1_sb = keep.tile([P, 4, K], BF16)
        wq_sb = keep.tile([P, 4, K], BF16)
        s_col = keep.tile([P, 4], F32)
        b1_raw = keep.tile([P, 4], BF16)
        qb_raw = keep.tile([P, 4], BF16)
        b1_col = keep.tile([P, 4], F32)
        qb_col = keep.tile([P, 4], F32)
        b1_bc = keep.tile([P, N], BF16)
        qb_bc = keep.tile([P, N], BF16)
        gb_rows = keep.tile([P, N], BF16)
        gb4 = keep.tile([P, 4, 2], F32)
        wq_perm = keep.tile([P, 4, K], BF16)
        ident_bf = keep.tile([P, P], BF16)
        eps = keep.tile([P, 1], F32)
        warm = keep.tile([P, 1], F32)
        w_codes = [keep.tile([P, N], U32, name="w_codes%d" % i, align_bytes=64) for i in range(2)]
        w_scales = [keep.tile([P, N], U8, name="w_scales%d" % i, align_bytes=64) for i in range(2)]

        s = {}

        def load_x(G):
            nc.sync.dma_start(out=raw[G][:], in_=xv[G])

        def spread(col):
            bt = pm.tile([P, 4, P], F32, name="acc")
            for t in range(4):
                nc.tensor.transpose(bt[:, t, :], col[:, t : t + 1].to_broadcast([P, P]), ident[:])
            return bt[:].rearrange("p t m -> p m t")

        def word_transposes(words, rows, xt):
            for i in range(2):
                for h in range(2):
                    nc.tensor.transpose(xt[:, h, P * i : P * (i + 1)], words[:, 256 * (rows + i) + h : 256 * (rows + i + 1) : 2], ident[:])
            return xt

        def w1_half(half):
            if half == 0:
                s["wg1"] = keep.tile([P, 4 * N], BF16, name="wg0", align_bytes=64)
            wt = pm.tile([P, 2, UNIT], F32, name="acc")
            word_transposes(w1_sb[:].rearrange("p c k -> p (c k)").bitcast(F32), 2 * half, wt)
            dst = s["wg1"][:, 1024 * half : 1024 * (half + 1)].bitcast(F32).rearrange("p (c h) -> p c h", h=2)
            copy = nc.scalar.copy if half == 0 else nc.vector.tensor_copy
            copy(out=dst, in_=wt[:].rearrange("p h c -> p c h"))

        def wq_half(half):
            if half == 0:
                s["wgq"] = keep.tile([P, 4 * N], BF16, name="wg1", align_bytes=64)
                gbt = px.tile([P, 4, P], BF16, name="xt")
                for t in range(4):
                    nc.tensor.transpose(gbt[:, t, :], gb_rows[:, P * t : P * (t + 1)], ident_bf[:])
                nc.scalar.copy(out=gb4[:], in_=gbt[:, :, 0:2])
            wt = px.tile([P, 4, UNIT], BF16, name="xt")
            for i in range(2):
                for t in range(4):
                    nc.tensor.transpose(wt[:, t, P * i : P * (i + 1)], wq_perm[:, 2 * half + i, P * t : P * (t + 1)], ident_bf[:])
            dst = s["wgq"][:, 1024 * half : 1024 * (half + 1)].rearrange("p (c t) -> p c t", t=4)
            nc.scalar.copy(out=dst, in_=wt[:].rearrange("p t c -> p c t"))

        def weight_quant(which, wg):
            nc.vector.quantize_mx(out=w_codes[which][:].bitcast(FP8X4), scales=w_scales[which][:], in_=wg[:])

        def A(u):
            xs = work.tile([P, 2 * K], BF16, name="xs", align_bytes=64)
            src = raw[u // 2][:, 2 * (u % 2) : 2 * (u % 2) + 2, :].rearrange("p j k -> p (j k)").bitcast(FP8)
            if u < 2:
                for i in range(2):
                    half = slice(K * i, K * (i + 1))
                    nc.vector.tensor_tensor(out=xs[:, half], in0=src[:, half], in1=scale2[:, 0, :], op=ALU.mult)
            else:
                nc.vector.tensor_tensor(out=xs[:], in0=src, in1=scale2[:].rearrange("p j k -> p (j k)"), op=ALU.mult)
            s["xs", u] = xs

        def XT(u):
            xt = px.tile([P, 2, UNIT], F32, name="xt")
            s["xt", u] = word_transposes(s.pop(("xs", u))[:].bitcast(F32), 0, xt)

        def T2(u):
            xt = s.pop(("xt", u))
            xg = work.tile([P, 4 * UNIT], BF16, name="xg", align_bytes=64)
            nc.scalar.copy(out=xg[:].bitcast(F32).rearrange("p (c h) -> p c h", h=2), in_=xt[:].rearrange("p h c -> p c h"))
            s["xg", u] = xg

        def QX(u):
            xg = s.pop(("xg", u))
            xc = work.tile([P, UNIT], U32, name="xc", align_bytes=64)
            xsc = work.tile([P, UNIT], U8, name="xsc", align_bytes=64)
            nc.vector.quantize_mx(out=xc[:].bitcast(FP8X4), scales=xsc[:], in_=xg[:])
            s["xq", u] = (xc, xsc)

        def MM(u, key, which, dst):
            codes, scales = s.pop((key, u))
            res = []
            for i in range(2):
                acc = pm.tile([P, N], F32, name="acc")
                cols = slice(P * i, P * (i + 1))
                nc.tensor.matmul_mx(out=acc[:], lhsT=codes[:, cols].bitcast(FP8X4), lhsT_scale=scales[:, cols], rhs=w_codes[which][:].bitcast(FP8X4), rhs_scale=w_scales[which][:], start=True, stop=True)
                res.append(acc)
            s[dst, u] = res

        def T4(u):
            accs = s.pop(("l", u))
            llm = outs.tile([P, 2, N], F32, name="llm")
            sums = small.tile([P, 2], F32, name="sums")
            for i in range(2):
                nc.vector.scalar_tensor_tensor(out=llm[:, i, :], in0=accs[i][:], scalar=1.0, in1=b1_bc[:], op0=ALU.mult, op1=ALU.add, accum_out=sums[:, i : i + 1])
            nc.sync.dma_start(out=o0[u // 2][:, 2 * (u % 2) : 2 * (u % 2) + 2, :], in_=llm[:])
            s["llm", u] = (llm, sums)

        def SQ(u):
            llm, sums = s["llm", u]
            ssq = small.tile([P, 2], F32, name="ssq")
            for i in range(2):
                junk = work.tile([P, N], BF16, name="junk")
                nc.scalar.activation(out=junk[:], in_=llm[:, i, :], func=ACT.Square, bias=sums[:, i : i + 1], scale=-float(N), accum_out=ssq[:, i : i + 1])
            s["ssq", u] = ssq

        def RS(u):
            rstd = small.tile([P, 2], F32, name="rstd")
            nc.scalar.activation(out=rstd[:], in_=s.pop(("ssq", u))[:], func=ACT.Abs_reciprocal_sqrt, bias=eps[:], scale=1.0 / N**3)
            s["rstd", u] = rstd

        def Z(u):
            llm, sums = s.pop(("llm", u))
            rstd = s.pop(("rstd", u))
            negmean = small.tile([P, 2], F32, name="negmean")
            nc.gpsimd.tensor_scalar(out=negmean[:], in0=sums[:], scalar1=-1.0 / N, scalar2=0.0, op0=ALU.mult, op1=ALU.add)
            z = work.tile([P, 2, 4, P], F32, name="z")
            for i in range(2):
                nc.gpsimd.tensor_scalar(out=z[:, i, :, :].rearrange("p t (b r) -> p t b r", r=8), in0=llm[:, i, :].rearrange("p (b t r) -> p t b r", t=4, r=8), scalar1=negmean[:, i : i + 1], scalar2=rstd[:, i : i + 1], op0=ALU.add, op1=ALU.mult)
            s["z", u] = z

        def ZT(u):
            z = s.pop(("z", u))
            res = []
            for a in range(2):
                zt = pz.tile([P, 2, UNIT], F32, name="zt")
                for tt in range(2):
                    for i in range(2):
                        nc.tensor.transpose(zt[:, tt, P * i : P * (i + 1)], z[:, i, 2 * a + tt, :], ident[:])
                res.append(zt)
            s["zt", u] = res

        def T7(u, ts):
            zts = s["zt", u]
            if 0 in ts:
                s["yp", u] = work.tile([P, 4, UNIT], BF16, name="yp", align_bytes=64)
            yp = s["yp", u]
            for t in ts:
                nc.scalar.activation(out=yp[:, t, :], in_=zts[t // 2][:, t % 2, :], func=ACT.Identity, bias=gb4[:, t, 1:2], scale=gb4[:, t, 0:1])

        def on_scalar(u):
            return u % 2 == 1 and u < 13

        def T8(u):
            yp = s.pop(("yp", u))
            yg = work.tile([P, 4 * UNIT], BF16, name="yg", align_bytes=64)
            dst, src = yg[:].rearrange("p (c t) -> p c t", t=4), yp[:].rearrange("p t c -> p c t")
            if on_scalar(u):
                nc.scalar.copy(out=dst, in_=src)
            else:
                nc.vector.tensor_copy(out=dst, in_=src)
            s["yg", u] = yg

        def QY(u):
            yg = s.pop(("yg", u))
            yc = work.tile([P, UNIT], U32, name="yc", align_bytes=64)
            ysc = work.tile([P, UNIT], U8, name="ysc", align_bytes=64)
            nc.vector.quantize_mx(out=yc[:].bitcast(FP8X4), scales=ysc[:], in_=yg[:])
            s["yq", u] = (yc, ysc)

        def T9(u):
            accs = s.pop(("q", u))
            qo = outs.tile([P, 2, N], F32, name="qo")
            for i in range(2):
                nc.vector.tensor_tensor(out=qo[:, i, :], in0=accs[i][:], in1=qb_bc[:], op=ALU.add)
                if u == UNITS - 1:
                    nc.sync.dma_start(out=o1[u // 2][:, 2 * (u % 2) + i, :], in_=qo[:, i, :])
            if u < UNITS - 1:
                nc.sync.dma_start(out=o1[u // 2][:, 2 * (u % 2) : 2 * (u % 2) + 2, :], in_=qo[:])

        def ok(u):
            return 0 <= u < UNITS

        with tc.manual_schedule():
            nc.scalar.dma_start(out=s_col[:], in_=x_scale.rearrange("a o (p t) -> p (a o t)", t=4))
            nc.scalar.dma_start(out=b1_raw[:], in_=b1.rearrange("(p t) -> p t", t=4))
            nc.scalar.dma_start(out=qb_raw[:], in_=qb.rearrange("(p t) -> p t", t=4))
            load_x(0)
            nc.sync.dma_start(out=w1_sb[:], in_=w1.rearrange("(c p) k -> p c k", p=P))
            load_x(1)
            nc.sync.dma_start(out=wq_sb[:], in_=wq.rearrange("(c p) k -> p c k", p=P))
            make_identity(nc, ident[:])
            nc.gpsimd.memset(warm[:], 1.0)
            nc.gpsimd.memset(gb_rows[:], 0.0)
            nc.gpsimd.memset(eps[:], EPS)
            make_identity(nc, ident_bf[:])
            for row, vec in ((0, g), (1, b)):
                nc.sync.dma_start(out=gb_rows[row : row + 1, :].rearrange("o (t b r) -> o t b r", t=4, r=8), in_=vec.rearrange("(o b t r) -> o t b r", o=1, t=4, r=8))
            for G in range(2, T // GROUP):
                load_x(G)
            nc.scalar.activation(out=warm[:], in_=warm[:], func=ACT.Abs_reciprocal_sqrt)
            nc.gpsimd.tensor_copy(out=b1_col[:], in_=b1_raw[:])
            nc.gpsimd.tensor_copy(out=qb_col[:], in_=qb_raw[:])
            for c in range(4):
                nc.gpsimd.tensor_scalar(
                    out=wq_perm[:, c, :].rearrange("p (t b r) -> p t b r", t=4, r=8),
                    in0=wq_sb[:, c, :].rearrange("p (b t r) -> p t b r", t=4, r=8),
                    scalar1=1.0, scalar2=0.0, op0=ALU.mult, op1=ALU.add)
            nc.scalar.copy(out=scale2[:, 0, :].rearrange("p (m t) -> p m t", t=4), in_=spread(s_col))
            w1_half(0)
            A(0)
            w1_half(1)
            b1_spread = spread(b1_col)
            XT(0)
            T2(0)
            nc.scalar.copy(out=b1_bc[:].rearrange("p (m t) -> p m t", t=4), in_=b1_spread)
            weight_quant(0, s.pop("wg1"))
            QX(0)
            MM(0, "xq", 0, "l")
            nc.scalar.copy(out=qb_bc[:].rearrange("p (m t) -> p m t", t=4), in_=spread(qb_col))
            nc.scalar.copy(out=scale2[:, 1, :], in_=scale2[:, 0, :])
            A(1)
            XT(1)
            T2(1)
            for i in range(UNITS + 3):
                if ok(i):
                    T4(i)
                if i == 0:
                    A(2)
                    XT(2)
                if ok(i - 2):
                    T8(i - 2)
                if ok(i - 1):
                    ZT(i - 1)
                if ok(i + 1):
                    QX(i + 1)
                if ok(i + 3):
                    A(i + 3)
                if ok(i + 1):
                    MM(i + 1, "xq", 0, "l")
                if ok(i):
                    SQ(i)
                    RS(i)
                if i == 2:
                    weight_quant(1, s.pop("wgq"))
                if ok(i - 2):
                    QY(i - 2)
                    MM(i - 2, "yq", 1, "q")
                if ok(i + 3):
                    XT(i + 3)
                if ok(i):
                    Z(i)
                if ok(i - 3):
                    T9(i - 3)
                if ok(i - 1):
                    T7(i - 1, (0, 1, 2, 3))
                if ok(i + 2) and i >= 0:
                    T2(i + 2)
                if i < 2:
                    wq_half(i)
